import numpy as np
import ml_dtypes


def mxq(x, axis, fmt="e4m3"):
    dtype, down = {"e4m3": (ml_dtypes.float8_e4m3fn, 7), "e5m2": (ml_dtypes.float8_e5m2, 14)}[fmt]
    v = np.moveaxis(np.asarray(x, np.float32).astype(ml_dtypes.bfloat16).astype(np.float64), axis, -1)
    blocks = v.reshape(v.shape[:-1] + (-1, 32))
    amax = np.abs(blocks).max(-1, keepdims=True)
    byte = np.maximum(np.where(amax > 0, np.frexp(amax)[1] - 1 + 127, 0) - down, 1)
    scale = np.exp2(byte - 127.0)
    codes = (blocks / scale).astype(np.float32).astype(dtype).astype(np.float64)
    return np.moveaxis((codes * scale).reshape(v.shape), -1, axis)


WIDE = False


def mx_kscale(k):
    if not WIDE:
        return np.ones(k)
    levels = np.array([10, -10, 5, -5, 0])
    a = np.random.permutation(np.resize(levels, k // 512 * 4)).reshape(k // 512, 4)
    idx = np.arange(k)
    return np.exp2(a[idx // 512, idx % 128 // 32])


BF16 = ml_dtypes.bfloat16


def bf(x):
    return np.asarray(x, np.float32).astype(BF16)


def f64(x):
    return np.asarray(x).astype(np.float64)


B, S, D, K, O, DEG, BLK = 4, 128, 1536, 1536, 2048, 6, 512
HALF = DEG // 2
STEP = K // DEG


def make_masks(lo, hi):
    rows = np.arange(K)
    deg_r = (rows * DEG) // K + 1
    degmask = (np.arange(1, DEG + 1)[:, None] <= deg_r[None, :]) * 1.0
    tri_l = np.tril(np.ones((K, D)))
    tri_u = np.triu(np.ones((K, D)))
    return np.stack([degmask[i][:, None] * (tri_l if i % 2 == 0 else tri_u) for i in range(lo, hi)])


def factor(zq, Wi, i):
    y = np.zeros((zq.shape[0], K))
    for j in range(K // BLK):
        a, b = max(j * BLK, i * STEP), (j + 1) * BLK
        c0, c1 = (0, min(b, D)) if i % 2 == 0 else (j * BLK, D)
        if a >= b or c0 >= c1:
            continue
        y[:, a:b] = zq[:, c0:c1] @ mxq(Wi[a:b, c0:c1], 1, "e4m3").T
    return y


def setup_inputs():
    s = mx_kscale(D)
    return {"z": bf(np.random.standard_normal((B, S, D)) * s),
            "U_lo": bf(np.random.standard_normal((HALF, K, D)) / np.sqrt(D) / s),
            "masks_lo": bf(make_masks(0, HALF))}


def reference(z, U_lo, masks_lo):
    zq = mxq(f64(z).reshape(-1, D), 1, "e4m3")
    W = f64(masks_lo) * f64(U_lo)
    out = factor(zq, W[0], 0)
    for i in range(1, HALF):
        out = factor(zq, W[i], i) * out + out
    return out

@@ -1,0 +1,204 @@
+from contextlib import ExitStack
+
+import concourse.bass as bass
+import concourse.mybir as mybir
+import concourse.tile as tile
+from concourse.masks import make_identity
+
+F32 = mybir.dt.float32
+BF16 = mybir.dt.bfloat16
+U32 = mybir.dt.uint32
+U8 = mybir.dt.uint8
+I32 = mybir.dt.int32
+FP8X4 = mybir.dt.float8_e4m3fn_x4
+ADD = mybir.AluOpType.add
+MULT = mybir.AluOpType.mult
+
+P = 128
+FEAT = 1536
+RANKS = 1536
+TOKENS = 512
+FACTORS = 3
+K_PASS = 512
+N_PASS = FEAT // K_PASS
+BLOCK = 512
+TOKEN_TILES = TOKENS // P
+LOWER = (True, False, True)
+
+ALIVE = 4063232
+FLOPS = 2 * TOKENS * ALIVE
+BYTES = TOKENS * FEAT * 2 + TOKENS * RANKS * 4 + 2 * 3049344
+
+PINNED = False
+
+
+def rank_tiles(i, rb):
+    return [r for r in range(4 * rb, 4 * rb + 4) if r >= 2 * i]
+
+
+def passes(i, rb):
+    return list(range(0, rb + 1)) if LOWER[i] else list(range(rb, N_PASS))
+
+
+def tile_span(i, r):
+    if LOWER[i]:
+        return 0, 256 * (r // 2 + 1)
+    return 256 * (r // 2), FEAT
+
+
+def alive_span(i, r):
+    if LOWER[i]:
+        return 0, P * (r + 1)
+    return P * r, FEAT
+
+
+def diagonal_masks(masks_lo, i, r0, n):
+    flat = masks_lo.rearrange("i r c -> (i r c)")
+    step = P * FEAT + P
+    start = i * RANKS * FEAT + r0 * step
+    assert start + n * step <= FACTORS * RANKS * FEAT
+    window = flat[start : start + n * step].rearrange("(t x) -> t x", x=step)
+    rows = window[:, 0 : P * FEAT].rearrange("t (p c) -> t p c", c=FEAT)
+    return rows[:, :, 0:P].rearrange("t p c -> p t c")
+
+
+def tile_cp_sparse_degree_lu_pa_kernel(tc, z, U_lo, masks_lo, out):
+    nc = tc.nc
+    groups = [(0, 0), (1, 0), (0, 1), (1, 1), (2, 1), (0, 2), (1, 2), (2, 2)]
+    last_factor = {0: 1, 1: 2, 2: 2}
+
+    with ExitStack() as ctx:
+        keep = ctx.enter_context(tc.tile_pool(name="keep", bufs=1))
+        stage = ctx.enter_context(tc.tile_pool(name="stage", bufs=4))
+        psum_t = ctx.enter_context(tc.psum_pool(name="psum_t", bufs=4))
+        psum_a = ctx.enter_context(tc.psum_pool(name="psum_a", bufs=4))
+        if PINNED:
+            ctx.enter_context(tc.manual_schedule())
+
+        ident = keep.tile([P, P], F32, name="ident")
+        make_identity(nc, ident[:])
+        zero = keep.tile([P, P], F32, name="zero")
+        nc.vector.memset(zero[:], 0.0)
+
+        z_sb = []
+        for tt in range(TOKEN_TILES):
+            zt = keep.tile([P, FEAT], BF16, name="z%d" % tt)
+            nc.sync.dma_start(out=zt[:], in_=z[tt, :, :])
+            z_sb.append(zt)
+        u_sb = {}
+        m_sb = {}
+        for i, rb in groups:
+            rs = rank_tiles(i, rb)
+            mt = keep.tile([P, len(rs), P], BF16, name="m%d_%d" % (i, rb))
+            if i == FACTORS - 1 and rb == 2:
+                nc.sync.dma_start(out=mt[:, 0:3, :], in_=diagonal_masks(masks_lo, i, rs[0], 3))
+                nc.sync.dma_start(out=mt[:, 3, :], in_=masks_lo[i, P * rs[3] : P * rs[3] + P, P * rs[3] : P * rs[3] + P])
+            else:
+                nc.sync.dma_start(out=mt[:], in_=diagonal_masks(masks_lo, i, rs[0], len(rs)))
+            m_sb[(i, rb)] = mt
+            for r in rs:
+                c0, c1 = tile_span(i, r)
+                a0, a1 = alive_span(i, r)
+                ut = keep.tile([P, c1 - c0], BF16, name="u%d_%d" % (i, r))
+                if a0 > c0:
+                    nc.vector.memset(ut[:, 0 : a0 - c0].bitcast(I32), 0)
+                if a1 < c1:
+                    nc.vector.memset(ut[:, a1 - c0 : c1 - c0].bitcast(I32), 0)
+                nc.sync.dma_start(out=ut[:, a0 - c0 : a1 - c0], in_=U_lo[i, P * r : P * r + P, a0:a1])
+                u_sb[(i, r)] = ut
+
+        zg = [keep.tile([P, 4 * TOKENS], BF16, name="zg%d" % g, align_bytes=64) for g in range(N_PASS)]
+        zc = [keep.tile([P, TOKENS], U32, name="zc%d" % g, align_bytes=64) for g in range(N_PASS)]
+        zs = [keep.tile([P, TOKENS], U8, name="zs%d" % g, align_bytes=64) for g in range(N_PASS)]
+        for h in range(TOKEN_TILES // 2):
+            banks = [psum_t.tile([P, 2, 256], F32, name="tpz%d" % g, tag="tp") for g in range(N_PASS)]
+            for a in range(2):
+                words = z_sb[2 * h + a][:].bitcast(F32)
+                for g in range(N_PASS):
+                    for u in range(2):
+                        w0 = 256 * g + P * u
+                        nc.tensor.transpose(banks[g][:, u, P * a : P * a + P], words[:, w0 : w0 + P], ident[:])
+            for g in range(N_PASS):
+                dst = zg[g][:].bitcast(F32).rearrange("p (r u) -> p r u", u=2)
+                src = banks[g][:].rearrange("p u r -> p r u")
+                if g == 1:
+                    nc.vector.tensor_copy(out=dst[:, 256 * h : 256 * h + 256, :], in_=src)
+                else:
+                    nc.scalar.copy(out=dst[:, 256 * h : 256 * h + 256, :], in_=src)
+        for g in range(N_PASS):
+            nc.vector.quantize_mx(out=zc[g][:].bitcast(FP8X4), scales=zs[g][:], in_=zg[g][:])
+
+        w_codes = {}
+        w_scales = {}
+        res = {}
+
+        def prepare(i, rb):
+            rs = rank_tiles(i, rb)
+            nr = P * len(rs)
+            for j, r in enumerate(rs):
+                c0, c1 = tile_span(i, r)
+                d0 = P * r - c0
+                ut = u_sb[(i, r)]
+                nc.vector.tensor_tensor(
+                    out=ut[:, d0 : d0 + P], in0=ut[:, d0 : d0 + P], in1=m_sb[(i, rb)][:, j, :], op=MULT
+                )
+            for g in passes(i, rb):
+                gr = stage.tile([P, 4 * nr], BF16, name="gr", tag="gr", align_bytes=64)
+                grw = gr[:].bitcast(F32).rearrange("p (r u) -> p r u", u=2)
+                for h in range(len(rs) // 2):
+                    tp = psum_t.tile([P, 2, 256], F32, name="tp", tag="tp")
+                    for a in range(2):
+                        r = rs[2 * h + a]
+                        c0, c1 = tile_span(i, r)
+                        for u in range(2):
+                            col = K_PASS * g + 256 * u
+                            if c0 <= col < c1:
+                                w0 = (col - c0) // 2
+                                src = u_sb[(i, r)][:].bitcast(F32)[:, w0 : w0 + P]
+                            else:
+                                src = zero[:]
+                            nc.tensor.transpose(tp[:, u, P * a : P * a + P], src, ident[:])
+                    nc.scalar.copy(out=grw[:, 256 * h : 256 * h + 256, :], in_=tp[:].rearrange("p u r -> p r u"))
+                wc = keep.tile([P, nr], U32, name="wc%d_%d_%d" % (i, rb, g), align_bytes=64)
+                ws = keep.tile([P, nr], U8, name="ws%d_%d_%d" % (i, rb, g), align_bytes=64)
+                nc.vector.quantize_mx(out=wc[:].bitcast(FP8X4), scales=ws[:], in_=gr[:])
+                w_codes[(i, rb, g)] = wc
+                w_scales[(i, rb, g)] = ws
+
+        def multiply(i, rb):
+            nr = P * len(rank_tiles(i, rb))
+            gs = passes(i, rb)
+            for tt in range(TOKEN_TILES):
+                acc = psum_a.tile([P, BLOCK], F32, name="acc", tag="acc")
+                for g in gs:
+                    nc.tensor.matmul_mx(
+                        out=acc[:, 0:nr],
+                        lhsT=zc[g][:, P * tt : P * tt + P].bitcast(FP8X4),
+                        lhsT_scale=zs[g][:, P * tt : P * tt + P],
+                        rhs=w_codes[(i, rb, g)][:].bitcast(FP8X4),
+                        rhs_scale=w_scales[(i, rb, g)][:],
+                        start=(g == gs[0]),
+                        stop=(g == gs[-1]),
+                    )
+                if i == 0:
+                    rt = keep.tile([P, BLOCK], F32, name="res%d_%d" % (rb, tt))
+                    res[(rb, tt)] = rt
+                    nc.scalar.copy(out=rt[:], in_=acc[:])
+                else:
+                    rt = res[(rb, tt)]
+                    nc.vector.scalar_tensor_tensor(
+                        out=rt[:, BLOCK - nr : BLOCK],
+                        in0=acc[:, 0:nr],
+                        scalar=1.0,
+                        in1=rt[:, BLOCK - nr : BLOCK],
+                        op0=ADD,
+                        op1=MULT,
+                    )
+                if i == last_factor[rb]:
+                    nc.sync.dma_start(out=out[P * tt : P * tt + P, BLOCK * rb : BLOCK * rb + BLOCK], in_=rt[:])
+
+        prepare(*groups[0])
+        for n in range(1, len(groups)):
+            prepare(*groups[n])
+            multiply(*groups[n - 1])
+        multiply(*groups[-1])

@@ -29,7 +29,7 @@ ALIVE = 4063232
 FLOPS = 2 * TOKENS * ALIVE
 BYTES = TOKENS * FEAT * 2 + TOKENS * RANKS * 4 + 2 * 3049344
 
-PINNED = False
+PINNED = True
 
 
 def rank_tiles(i, rb):

@@ -1,8 +1,6 @@
 from contextlib import ExitStack
 
-import concourse.bass as bass
 import concourse.mybir as mybir
-import concourse.tile as tile
 from concourse.masks import make_identity
 
 F32 = mybir.dt.float32
@@ -18,7 +16,6 @@ P = 128
 FEAT = 1536
 RANKS = 1536
 TOKENS = 512
-FACTORS = 3
 K_PASS = 512
 N_PASS = FEAT // K_PASS
 BLOCK = 512
@@ -30,6 +27,10 @@ FLOPS = 2 * TOKENS * ALIVE
 BYTES = TOKENS * FEAT * 2 + TOKENS * RANKS * 4 + 2 * 3049344
 
 PINNED = True
+RUN = 4
+LAG = 2
+GROUPS = ((0, 0), (0, 1), (2, 1), (1, 1), (1, 0), (0, 2), (1, 2), (2, 2))
+Z_BEFORE = {0: 0, 1: 1, 3: 2}
 
 
 def rank_tiles(i, rb):
@@ -52,20 +53,14 @@ def alive_span(i, r):
     return P * r, FEAT
 
 
-def diagonal_masks(masks_lo, i, r0, n):
-    flat = masks_lo.rearrange("i r c -> (i r c)")
-    step = P * FEAT + P
-    start = i * RANKS * FEAT + r0 * step
-    assert start + n * step <= FACTORS * RANKS * FEAT
-    window = flat[start : start + n * step].rearrange("(t x) -> t x", x=step)
-    rows = window[:, 0 : P * FEAT].rearrange("t (p c) -> t p c", c=FEAT)
-    return rows[:, :, 0:P].rearrange("t p c -> p t c")
-
-
 def tile_cp_sparse_degree_lu_pa_kernel(tc, z, U_lo, masks_lo, out):
     nc = tc.nc
-    groups = [(0, 0), (1, 0), (0, 1), (1, 1), (2, 1), (0, 2), (1, 2), (2, 2)]
-    last_factor = {0: 1, 1: 2, 2: 2}
+    first_factor = {}
+    last_factor = {}
+    for i, rb in GROUPS:
+        if rb not in first_factor:
+            first_factor[rb] = i
+        last_factor[rb] = i
 
     with ExitStack() as ctx:
         keep = ctx.enter_context(tc.tile_pool(name="keep", bufs=1))
@@ -77,26 +72,25 @@ def tile_cp_sparse_degree_lu_pa_kernel(tc, z, U_lo, masks_lo, out):
 
         ident = keep.tile([P, P], F32, name="ident")
         make_identity(nc, ident[:])
-        zero = keep.tile([P, P], F32, name="zero")
-        nc.vector.memset(zero[:], 0.0)
 
-        z_sb = []
-        for tt in range(TOKEN_TILES):
-            zt = keep.tile([P, FEAT], BF16, name="z%d" % tt)
-            nc.sync.dma_start(out=zt[:], in_=z[tt, :, :])
-            z_sb.append(zt)
+        tri = {}
+        for lower, i, r in ((True, 0, 0), (False, 1, 2)):
+            mt = keep.tile([P, P], BF16, name="tri%d" % i)
+            nc.sync.dma_start(out=mt[:], in_=masks_lo[i, P * r : P * r + P, P * r : P * r + P])
+            tri[lower] = mt
+        z_sb = {}
         u_sb = {}
-        m_sb = {}
-        for i, rb in groups:
-            rs = rank_tiles(i, rb)
-            mt = keep.tile([P, len(rs), P], BF16, name="m%d_%d" % (i, rb))
-            if i == FACTORS - 1 and rb == 2:
-                nc.sync.dma_start(out=mt[:, 0:3, :], in_=diagonal_masks(masks_lo, i, rs[0], 3))
-                nc.sync.dma_start(out=mt[:, 3, :], in_=masks_lo[i, P * rs[3] : P * rs[3] + P, P * rs[3] : P * rs[3] + P])
-            else:
-                nc.sync.dma_start(out=mt[:], in_=diagonal_masks(masks_lo, i, rs[0], len(rs)))
-            m_sb[(i, rb)] = mt
-            for r in rs:
+        for n, (i, rb) in enumerate(GROUPS):
+            if n in Z_BEFORE:
+                g = Z_BEFORE[n]
+                for h in range(2):
+                    zt = keep.tile([P, 2, K_PASS], BF16, name="z%d_%d" % (g, h))
+                    nc.sync.dma_start(
+                        out=zt[:],
+                        in_=z[2 * h : 2 * h + 2, :, K_PASS * g : K_PASS * g + K_PASS].rearrange("t p c -> p t c"),
+                    )
+                    z_sb[(g, h)] = zt
+            for r in rank_tiles(i, rb):
                 c0, c1 = tile_span(i, r)
                 a0, a1 = alive_span(i, r)
                 ut = keep.tile([P, c1 - c0], BF16, name="u%d_%d" % (i, r))
@@ -107,80 +101,149 @@ def tile_cp_sparse_degree_lu_pa_kernel(tc, z, U_lo, masks_lo, out):
                 nc.sync.dma_start(out=ut[:, a0 - c0 : a1 - c0], in_=U_lo[i, P * r : P * r + P, a0:a1])
                 u_sb[(i, r)] = ut
 
-        zg = [keep.tile([P, 4 * TOKENS], BF16, name="zg%d" % g, align_bytes=64) for g in range(N_PASS)]
-        zc = [keep.tile([P, TOKENS], U32, name="zc%d" % g, align_bytes=64) for g in range(N_PASS)]
-        zs = [keep.tile([P, TOKENS], U8, name="zs%d" % g, align_bytes=64) for g in range(N_PASS)]
-        for h in range(TOKEN_TILES // 2):
-            banks = [psum_t.tile([P, 2, 256], F32, name="tpz%d" % g, tag="tp") for g in range(N_PASS)]
-            for a in range(2):
-                words = z_sb[2 * h + a][:].bitcast(F32)
-                for g in range(N_PASS):
-                    for u in range(2):
-                        w0 = 256 * g + P * u
-                        nc.tensor.transpose(banks[g][:, u, P * a : P * a + P], words[:, w0 : w0 + P], ident[:])
-            for g in range(N_PASS):
-                dst = zg[g][:].bitcast(F32).rearrange("p (r u) -> p r u", u=2)
-                src = banks[g][:].rearrange("p u r -> p r u")
-                if g == 1:
-                    nc.vector.tensor_copy(out=dst[:, 256 * h : 256 * h + 256, :], in_=src)
+        banks = []
+        for n, (i, rb) in enumerate(GROUPS):
+            if n in Z_BEFORE:
+                banks.append(("z", n, Z_BEFORE[n], 0, False))
+                banks.append(("z", n, Z_BEFORE[n], 1, True))
+            gs = passes(i, rb)
+            if not LOWER[i]:
+                gs = list(reversed(gs))
+            nb = len(rank_tiles(i, rb)) // 2
+            for g in gs:
+                for h in range(nb):
+                    banks.append(("w", n, g, h, h == nb - 1))
+        runs = [banks[k : k + RUN] for k in range(0, len(banks), RUN)]
+        run_of_group = {}
+        run_of_z = {}
+        for k, bank_run in enumerate(runs):
+            for kind, n, g, h, done in bank_run:
+                if kind == "z":
+                    run_of_z[g] = k
                 else:
-                    nc.scalar.copy(out=dst[:, 256 * h : 256 * h + 256, :], in_=src)
-        for g in range(N_PASS):
-            nc.vector.quantize_mx(out=zc[g][:].bitcast(FP8X4), scales=zs[g][:], in_=zg[g][:])
+                    run_of_group[n] = k
 
+        def alive_planes(i, rb, g, h):
+            rs = rank_tiles(i, rb)
+            c0, c1 = tile_span(i, rs[2 * h])
+            d0, d1 = tile_span(i, rs[2 * h + 1])
+            return [u for u in range(2) if min(c0, d0) <= K_PASS * g + 256 * u < max(c1, d1)]
+
+        fixed_gr = {}
+        for n, (i, rb) in enumerate(GROUPS):
+            nb = len(rank_tiles(i, rb)) // 2
+            for g in passes(i, rb):
+                for h in range(nb):
+                    if len(alive_planes(i, rb, g, h)) == 1:
+                        gt = keep.tile([P, 1024 * nb], BF16, name="gf%d_%d" % (n, g), align_bytes=64)
+                        nc.vector.memset(gt[:, 1024 * h : 1024 * h + 1024].bitcast(I32), 0)
+                        fixed_gr[(n, g)] = gt
+
+        zg = {}
+        zc = {}
+        zs = {}
+        gr_of = {}
         w_codes = {}
         w_scales = {}
         res = {}
+        tp_of = {}
+        masked = set()
 
-        def prepare(i, rb):
+        def mask_run(k):
+            if k >= len(runs):
+                return
+            for kind, n, g, h, done in runs[k]:
+                if kind == "w" and n not in masked:
+                    masked.add(n)
+                    i, rb = GROUPS[n]
+                    for r in rank_tiles(i, rb):
+                        d0 = P * r - tile_span(i, r)[0]
+                        ut = u_sb[(i, r)]
+                        nc.vector.tensor_tensor(
+                            out=ut[:, d0 : d0 + P], in0=ut[:, d0 : d0 + P], in1=tri[LOWER[i]][:], op=MULT
+                        )
+
+        def transpose_bank(bank):
+            kind, n, g, h, done = bank
+            tp = psum_t.tile([P, 2, 256], F32, name="tp", tag="tp")
+            tp_of[bank] = tp
+            if kind == "z":
+                for a in range(2):
+                    words = z_sb[(g, h)][:, a, :].bitcast(F32)
+                    for u in range(2):
+                        nc.tensor.transpose(tp[:, u, P * a : P * a + P], words[:, P * u : P * u + P], ident[:])
+                return
+            i, rb = GROUPS[n]
             rs = rank_tiles(i, rb)
-            nr = P * len(rs)
-            for j, r in enumerate(rs):
-                c0, c1 = tile_span(i, r)
-                d0 = P * r - c0
-                ut = u_sb[(i, r)]
-                nc.vector.tensor_tensor(
-                    out=ut[:, d0 : d0 + P], in0=ut[:, d0 : d0 + P], in1=m_sb[(i, rb)][:, j, :], op=MULT
-                )
-            for g in passes(i, rb):
-                gr = stage.tile([P, 4 * nr], BF16, name="gr", tag="gr", align_bytes=64)
-                grw = gr[:].bitcast(F32).rearrange("p (r u) -> p r u", u=2)
-                for h in range(len(rs) // 2):
-                    tp = psum_t.tile([P, 2, 256], F32, name="tp", tag="tp")
-                    for a in range(2):
-                        r = rs[2 * h + a]
-                        c0, c1 = tile_span(i, r)
-                        for u in range(2):
-                            col = K_PASS * g + 256 * u
-                            if c0 <= col < c1:
-                                w0 = (col - c0) // 2
-                                src = u_sb[(i, r)][:].bitcast(F32)[:, w0 : w0 + P]
-                            else:
-                                src = zero[:]
-                            nc.tensor.transpose(tp[:, u, P * a : P * a + P], src, ident[:])
-                    nc.scalar.copy(out=grw[:, 256 * h : 256 * h + 256, :], in_=tp[:].rearrange("p u r -> p r u"))
-                wc = keep.tile([P, nr], U32, name="wc%d_%d_%d" % (i, rb, g), align_bytes=64)
-                ws = keep.tile([P, nr], U8, name="ws%d_%d_%d" % (i, rb, g), align_bytes=64)
-                nc.vector.quantize_mx(out=wc[:].bitcast(FP8X4), scales=ws[:], in_=gr[:])
-                w_codes[(i, rb, g)] = wc
-                w_scales[(i, rb, g)] = ws
+            for plane, u in enumerate(alive_planes(i, rb, g, h)):
+                for a in range(2):
+                    r = rs[2 * h + a]
+                    w0 = (K_PASS * g + 256 * u - tile_span(i, r)[0]) // 2
+                    nc.tensor.transpose(
+                        tp[:, plane, P * a : P * a + P], u_sb[(i, r)][:].bitcast(F32)[:, w0 : w0 + P], ident[:]
+                    )
 
-        def multiply(i, rb):
+        def copy_bank(bank):
+            kind, n, g, h, done = bank
+            tp = tp_of[bank]
+            if kind == "z":
+                if h == 0:
+                    zg[g] = keep.tile([P, 4 * TOKENS], BF16, name="zg%d" % g, align_bytes=64)
+                dst = zg[g][:].bitcast(F32).rearrange("p (r u) -> p r u", u=2)
+                nc.scalar.copy(out=dst[:, 256 * h : 256 * h + 256, :], in_=tp[:].rearrange("p u r -> p r u"))
+                return
+            i, rb = GROUPS[n]
+            nb = len(rank_tiles(i, rb)) // 2
+            if h == 0:
+                if (n, g) in fixed_gr:
+                    gr_of[(n, g)] = fixed_gr[(n, g)]
+                else:
+                    gr_of[(n, g)] = stage.tile([P, 1024 * nb], BF16, name="gr", tag="gr", align_bytes=64)
+            dst = gr_of[(n, g)][:].bitcast(F32).rearrange("p (r u) -> p r u", u=2)
+            planes = alive_planes(i, rb, g, h)
+            if len(planes) == 2:
+                nc.scalar.copy(out=dst[:, 256 * h : 256 * h + 256, :], in_=tp[:].rearrange("p u r -> p r u"))
+            else:
+                u = planes[0]
+                nc.scalar.copy(
+                    out=dst[:, 256 * h : 256 * h + 256, u : u + 1], in_=tp[:, 0:1, :].rearrange("p u r -> p r u")
+                )
+
+        def quantise(bank):
+            kind, n, g, h, done = bank
+            if kind == "z":
+                zc[g] = keep.tile([P, TOKENS], U32, name="zc%d" % g, align_bytes=64)
+                zs[g] = keep.tile([P, TOKENS], U8, name="zs%d" % g, align_bytes=64)
+                nc.vector.quantize_mx(out=zc[g][:].bitcast(FP8X4), scales=zs[g][:], in_=zg[g][:])
+                return
+            nr = P * len(rank_tiles(*GROUPS[n]))
+            wc = keep.tile([P, nr], U32, name="wc%d_%d" % (n, g), align_bytes=64)
+            ws = keep.tile([P, nr], U8, name="ws%d_%d" % (n, g), align_bytes=64)
+            nc.vector.quantize_mx(out=wc[:].bitcast(FP8X4), scales=ws[:], in_=gr_of[(n, g)][:])
+            w_codes[(n, g)] = wc
+            w_scales[(n, g)] = ws
+
+        def multiply(n, pending):
+            i, rb = GROUPS[n]
             nr = P * len(rank_tiles(i, rb))
             gs = passes(i, rb)
+            accs = []
             for tt in range(TOKEN_TILES):
                 acc = psum_a.tile([P, BLOCK], F32, name="acc", tag="acc")
+                accs.append(acc)
                 for g in gs:
                     nc.tensor.matmul_mx(
                         out=acc[:, 0:nr],
                         lhsT=zc[g][:, P * tt : P * tt + P].bitcast(FP8X4),
                         lhsT_scale=zs[g][:, P * tt : P * tt + P],
-                        rhs=w_codes[(i, rb, g)][:].bitcast(FP8X4),
-                        rhs_scale=w_scales[(i, rb, g)][:],
+                        rhs=w_codes[(n, g)][:].bitcast(FP8X4),
+                        rhs_scale=w_scales[(n, g)][:],
                         start=(g == gs[0]),
                         stop=(g == gs[-1]),
                     )
-                if i == 0:
+            for tt in range(TOKEN_TILES):
+                acc = accs[tt]
+                if i == first_factor[rb]:
                     rt = keep.tile([P, BLOCK], F32, name="res%d_%d" % (rb, tt))
                     res[(rb, tt)] = rt
                     nc.scalar.copy(out=rt[:], in_=acc[:])
@@ -196,9 +259,30 @@ def tile_cp_sparse_degree_lu_pa_kernel(tc, z, U_lo, masks_lo, out):
                     )
                 if i == last_factor[rb]:
                     nc.sync.dma_start(out=out[P * tt : P * tt + P, BLOCK * rb : BLOCK * rb + BLOCK], in_=rt[:])
+                if tt < len(pending):
+                    quantise(pending[tt])
+            for bank in pending[TOKEN_TILES:]:
+                quantise(bank)
 
-        prepare(*groups[0])
-        for n in range(1, len(groups)):
-            prepare(*groups[n])
-            multiply(*groups[n - 1])
-        multiply(*groups[-1])
+        mask_run(0)
+        d_next = 0
+        for k, bank_run in enumerate(runs):
+            for bank in bank_run:
+                transpose_bank(bank)
+            mask_run(k + 1)
+            for bank in bank_run:
+                copy_bank(bank)
+            pending = [bank for bank in bank_run if bank[4]]
+            ready = False
+            if d_next < len(GROUPS):
+                need = max([run_of_group[d_next]] + [run_of_z[g] for g in passes(*GROUPS[d_next])])
+                ready = need <= k - LAG
+            if ready:
+                multiply(d_next, pending)
+                d_next += 1
+            else:
+                for bank in pending:
+                    quantise(bank)
+        while d_next < len(GROUPS):
+            multiply(d_next, [])
+            d_next += 1

@@ -74,10 +74,6 @@ def tile_cp_sparse_degree_lu_pa_kernel(tc, z, U_lo, masks_lo, out):
         make_identity(nc, ident[:])
 
         tri = {}
-        for lower, i, r in ((True, 0, 0), (False, 1, 2)):
-            mt = keep.tile([P, P], BF16, name="tri%d" % i)
-            nc.sync.dma_start(out=mt[:], in_=masks_lo[i, P * r : P * r + P, P * r : P * r + P])
-            tri[lower] = mt
         z_sb = {}
         u_sb = {}
         for n, (i, rb) in enumerate(GROUPS):
@@ -90,6 +86,11 @@ def tile_cp_sparse_degree_lu_pa_kernel(tc, z, U_lo, masks_lo, out):
                         in_=z[2 * h : 2 * h + 2, :, K_PASS * g : K_PASS * g + K_PASS].rearrange("t p c -> p t c"),
                     )
                     z_sb[(g, h)] = zt
+            if n == 0:
+                for lower, mi, mr in ((True, 0, 0), (False, 1, 2)):
+                    mt = keep.tile([P, P], BF16, name="tri%d" % mi)
+                    nc.sync.dma_start(out=mt[:], in_=masks_lo[mi, P * mr : P * mr + P, P * mr : P * mr + P])
+                    tri[lower] = mt
             for r in rank_tiles(i, rb):
                 c0, c1 = tile_span(i, r)
                 a0, a1 = alive_span(i, r)
@@ -113,7 +114,7 @@ def tile_cp_sparse_degree_lu_pa_kernel(tc, z, U_lo, masks_lo, out):
             for g in gs:
                 for h in range(nb):
                     banks.append(("w", n, g, h, h == nb - 1))
-        runs = [banks[k : k + RUN] for k in range(0, len(banks), RUN)]
+        runs = [banks[0:4], banks[4:6]] + [banks[k : k + RUN] for k in range(6, len(banks), RUN)]
         run_of_group = {}
         run_of_z = {}
         for k, bank_run in enumerate(runs):
@@ -223,66 +224,85 @@ def tile_cp_sparse_degree_lu_pa_kernel(tc, z, U_lo, masks_lo, out):
             w_codes[(n, g)] = wc
             w_scales[(n, g)] = ws
 
-        def multiply(n, pending):
-            i, rb = GROUPS[n]
-            nr = P * len(rank_tiles(i, rb))
-            gs = passes(i, rb)
-            accs = []
-            for tt in range(TOKEN_TILES):
-                acc = psum_a.tile([P, BLOCK], F32, name="acc", tag="acc")
-                accs.append(acc)
-                for g in gs:
-                    nc.tensor.matmul_mx(
-                        out=acc[:, 0:nr],
-                        lhsT=zc[g][:, P * tt : P * tt + P].bitcast(FP8X4),
-                        lhsT_scale=zs[g][:, P * tt : P * tt + P],
-                        rhs=w_codes[(n, g)][:].bitcast(FP8X4),
-                        rhs_scale=w_scales[(n, g)][:],
-                        start=(g == gs[0]),
-                        stop=(g == gs[-1]),
-                    )
-            for tt in range(TOKEN_TILES):
-                acc = accs[tt]
-                if i == first_factor[rb]:
-                    rt = keep.tile([P, BLOCK], F32, name="res%d_%d" % (rb, tt))
-                    res[(rb, tt)] = rt
-                    nc.scalar.copy(out=rt[:], in_=acc[:])
-                else:
+        def cuts(n, tt):
+            nr = P * len(rank_tiles(*GROUPS[n]))
+            if n == len(GROUPS) - 1 and tt == TOKEN_TILES - 1:
+                return [(0, nr // 2), (nr // 2, nr // 2)]
+            return [(0, nr)]
+
+        def multiply(due, pending):
+            accs = {}
+            for n in due:
+                i, rb = GROUPS[n]
+                gs = passes(i, rb)
+                for tt in range(TOKEN_TILES):
+                    acc = psum_a.tile([P, BLOCK], F32, name="acc", tag="acc")
+                    accs[(n, tt)] = acc
+                    for c0, width in cuts(n, tt):
+                        for g in gs:
+                            nc.tensor.matmul_mx(
+                                out=acc[:, c0 : c0 + width],
+                                lhsT=zc[g][:, P * tt : P * tt + P].bitcast(FP8X4),
+                                lhsT_scale=zs[g][:, P * tt : P * tt + P],
+                                rhs=w_codes[(n, g)][:, c0 : c0 + width].bitcast(FP8X4),
+                                rhs_scale=w_scales[(n, g)][:, c0 : c0 + width],
+                                start=(g == gs[0]),
+                                stop=(g == gs[-1]),
+                            )
+            served = 0
+            for n in due:
+                i, rb = GROUPS[n]
+                nr = P * len(rank_tiles(i, rb))
+                for tt in range(TOKEN_TILES):
+                    acc = accs[(n, tt)]
+                    if i == first_factor[rb]:
+                        res[(rb, tt)] = keep.tile([P, BLOCK], F32, name="res%d_%d" % (rb, tt))
                     rt = res[(rb, tt)]
-                    nc.vector.scalar_tensor_tensor(
-                        out=rt[:, BLOCK - nr : BLOCK],
-                        in0=acc[:, 0:nr],
-                        scalar=1.0,
-                        in1=rt[:, BLOCK - nr : BLOCK],
-                        op0=ADD,
-                        op1=MULT,
-                    )
-                if i == last_factor[rb]:
-                    nc.sync.dma_start(out=out[P * tt : P * tt + P, BLOCK * rb : BLOCK * rb + BLOCK], in_=rt[:])
-                if tt < len(pending):
-                    quantise(pending[tt])
-            for bank in pending[TOKEN_TILES:]:
+                    for c0, width in cuts(n, tt):
+                        r0 = BLOCK - nr + c0
+                        if i != first_factor[rb]:
+                            nc.vector.scalar_tensor_tensor(
+                                out=rt[:, r0 : r0 + width],
+                                in0=acc[:, c0 : c0 + width],
+                                scalar=1.0,
+                                in1=rt[:, r0 : r0 + width],
+                                op0=ADD,
+                                op1=MULT,
+                            )
+                        elif rb == 0:
+                            nc.vector.tensor_copy(out=rt[:, r0 : r0 + width], in_=acc[:, c0 : c0 + width])
+                        else:
+                            nc.scalar.copy(out=rt[:, r0 : r0 + width], in_=acc[:, c0 : c0 + width])
+                        if i == last_factor[rb]:
+                            s0 = 0 if c0 == 0 else r0
+                            nc.sync.dma_start(
+                                out=out[P * tt : P * tt + P, BLOCK * rb + s0 : BLOCK * rb + r0 + width],
+                                in_=rt[:, s0 : r0 + width],
+                            )
+                    if served < len(pending):
+                        quantise(pending[served])
+                        served += 1
+            for bank in pending[served:]:
                 quantise(bank)
 
+        d_after = []
+        for n, (i, rb) in enumerate(GROUPS):
+            need = max([run_of_group[n]] + [run_of_z[g] for g in passes(i, rb)])
+            d_after.append(max(d_after[-1:] + [need + (1 if n == 0 else LAG)]))
+
         mask_run(0)
-        d_next = 0
         for k, bank_run in enumerate(runs):
             for bank in bank_run:
                 transpose_bank(bank)
-            mask_run(k + 1)
+            if k > 0:
+                mask_run(k + 1)
             for bank in bank_run:
                 copy_bank(bank)
             pending = [bank for bank in bank_run if bank[4]]
-            ready = False
-            if d_next < len(GROUPS):
-                need = max([run_of_group[d_next]] + [run_of_z[g] for g in passes(*GROUPS[d_next])])
-                ready = need <= k - LAG
-            if ready:
-                multiply(d_next, pending)
-                d_next += 1
-            else:
+            if k == 0:
                 for bank in pending:
                     quantise(bank)
-        while d_next < len(GROUPS):
-            multiply(d_next, [])
-            d_next += 1
+                pending = []
+                mask_run(1)
+            multiply([n for n in range(len(GROUPS)) if d_after[n] == k], pending)
+        multiply([n for n in range(len(GROUPS)) if d_after[n] >= len(runs)], [])

@@ -53,6 +53,18 @@ def alive_span(i, r):
     return P * r, FEAT
 
 
+def group_window(i, rb):
+    if LOWER[i]:
+        return 0, BLOCK * (rb + 1)
+    lo = P * rank_tiles(i, rb)[0]
+    return lo, FEAT - lo
+
+
+def place(i, rb, j, c):
+    lo, width = group_window(i, rb)
+    return (BLOCK if LOWER[i] else 0) + j * width + c - lo
+
+
 def tile_cp_sparse_degree_lu_pa_kernel(tc, z, U_lo, masks_lo, out):
     nc = tc.nc
     first_factor = {}
@@ -74,6 +86,10 @@ def tile_cp_sparse_degree_lu_pa_kernel(tc, z, U_lo, masks_lo, out):
         make_identity(nc, ident[:])
 
         tri = {}
+        for lower, i, r in ((True, 0, 0), (False, 1, 2)):
+            mt = keep.tile([P, P], BF16, name="tri%d" % i)
+            nc.sync.dma_start(out=mt[:], in_=masks_lo[i, P * r : P * r + P, P * r : P * r + P])
+            tri[lower] = mt
         z_sb = {}
         u_sb = {}
         for n, (i, rb) in enumerate(GROUPS):
@@ -86,21 +102,19 @@ def tile_cp_sparse_degree_lu_pa_kernel(tc, z, U_lo, masks_lo, out):
                         in_=z[2 * h : 2 * h + 2, :, K_PASS * g : K_PASS * g + K_PASS].rearrange("t p c -> p t c"),
                     )
                     z_sb[(g, h)] = zt
-            if n == 0:
-                for lower, mi, mr in ((True, 0, 0), (False, 1, 2)):
-                    mt = keep.tile([P, P], BF16, name="tri%d" % mi)
-                    nc.sync.dma_start(out=mt[:], in_=masks_lo[mi, P * mr : P * mr + P, P * mr : P * mr + P])
-                    tri[lower] = mt
-            for r in rank_tiles(i, rb):
+            rs = rank_tiles(i, rb)
+            ut = keep.tile([P, len(rs) * (group_window(i, rb)[1] + P)], BF16, name="u%d_%d" % (i, rb))
+            u_sb[(i, rb)] = ut
+            for j, r in enumerate(rs):
                 c0, c1 = tile_span(i, r)
                 a0, a1 = alive_span(i, r)
-                ut = keep.tile([P, c1 - c0], BF16, name="u%d_%d" % (i, r))
                 if a0 > c0:
-                    nc.vector.memset(ut[:, 0 : a0 - c0].bitcast(I32), 0)
+                    nc.vector.memset(ut[:, place(i, rb, j, c0) : place(i, rb, j, a0)].bitcast(I32), 0)
                 if a1 < c1:
-                    nc.vector.memset(ut[:, a1 - c0 : c1 - c0].bitcast(I32), 0)
-                nc.sync.dma_start(out=ut[:, a0 - c0 : a1 - c0], in_=U_lo[i, P * r : P * r + P, a0:a1])
-                u_sb[(i, r)] = ut
+                    nc.vector.memset(ut[:, place(i, rb, j, a1) : place(i, rb, j, c1)].bitcast(I32), 0)
+                nc.sync.dma_start(
+                    out=ut[:, place(i, rb, j, a0) : place(i, rb, j, a1)], in_=U_lo[i, P * r : P * r + P, a0:a1]
+                )
 
         banks = []
         for n, (i, rb) in enumerate(GROUPS):
@@ -114,7 +128,7 @@ def tile_cp_sparse_degree_lu_pa_kernel(tc, z, U_lo, masks_lo, out):
             for g in gs:
                 for h in range(nb):
                     banks.append(("w", n, g, h, h == nb - 1))
-        runs = [banks[0:4], banks[4:6]] + [banks[k : k + RUN] for k in range(6, len(banks), RUN)]
+        runs = [banks[k : k + RUN] for k in range(0, len(banks), RUN)]
         run_of_group = {}
         run_of_z = {}
         for k, bank_run in enumerate(runs):
@@ -157,12 +171,13 @@ def tile_cp_sparse_degree_lu_pa_kernel(tc, z, U_lo, masks_lo, out):
                 if kind == "w" and n not in masked:
                     masked.add(n)
                     i, rb = GROUPS[n]
-                    for r in rank_tiles(i, rb):
-                        d0 = P * r - tile_span(i, r)[0]
-                        ut = u_sb[(i, r)]
-                        nc.vector.tensor_tensor(
-                            out=ut[:, d0 : d0 + P], in0=ut[:, d0 : d0 + P], in1=tri[LOWER[i]][:], op=MULT
-                        )
+                    nj = len(rank_tiles(i, rb))
+                    width = group_window(i, rb)[1]
+                    d0 = width if LOWER[i] else 0
+                    diag = u_sb[(i, rb)][:].rearrange("p (j x) -> p j x", x=width + P)[:, :, d0 : d0 + P]
+                    nc.vector.tensor_tensor(
+                        out=diag, in0=diag, in1=tri[LOWER[i]][:].unsqueeze(1).to_broadcast([P, nj, P]), op=MULT
+                    )
 
         def transpose_bank(bank):
             kind, n, g, h, done = bank
@@ -178,10 +193,9 @@ def tile_cp_sparse_degree_lu_pa_kernel(tc, z, U_lo, masks_lo, out):
             rs = rank_tiles(i, rb)
             for plane, u in enumerate(alive_planes(i, rb, g, h)):
                 for a in range(2):
-                    r = rs[2 * h + a]
-                    w0 = (K_PASS * g + 256 * u - tile_span(i, r)[0]) // 2
+                    w0 = place(i, rb, 2 * h + a, K_PASS * g + 256 * u) // 2
                     nc.tensor.transpose(
-                        tp[:, plane, P * a : P * a + P], u_sb[(i, r)][:].bitcast(F32)[:, w0 : w0 + P], ident[:]
+                        tp[:, plane, P * a : P * a + P], u_sb[(i, rb)][:].bitcast(F32)[:, w0 : w0 + P], ident[:]
                     )
 
         def copy_bank(bank):
@@ -224,85 +238,66 @@ def tile_cp_sparse_degree_lu_pa_kernel(tc, z, U_lo, masks_lo, out):
             w_codes[(n, g)] = wc
             w_scales[(n, g)] = ws
 
-        def cuts(n, tt):
-            nr = P * len(rank_tiles(*GROUPS[n]))
-            if n == len(GROUPS) - 1 and tt == TOKEN_TILES - 1:
-                return [(0, nr // 2), (nr // 2, nr // 2)]
-            return [(0, nr)]
-
-        def multiply(due, pending):
-            accs = {}
-            for n in due:
-                i, rb = GROUPS[n]
-                gs = passes(i, rb)
-                for tt in range(TOKEN_TILES):
-                    acc = psum_a.tile([P, BLOCK], F32, name="acc", tag="acc")
-                    accs[(n, tt)] = acc
-                    for c0, width in cuts(n, tt):
-                        for g in gs:
-                            nc.tensor.matmul_mx(
-                                out=acc[:, c0 : c0 + width],
-                                lhsT=zc[g][:, P * tt : P * tt + P].bitcast(FP8X4),
-                                lhsT_scale=zs[g][:, P * tt : P * tt + P],
-                                rhs=w_codes[(n, g)][:, c0 : c0 + width].bitcast(FP8X4),
-                                rhs_scale=w_scales[(n, g)][:, c0 : c0 + width],
-                                start=(g == gs[0]),
-                                stop=(g == gs[-1]),
-                            )
-            served = 0
-            for n in due:
-                i, rb = GROUPS[n]
-                nr = P * len(rank_tiles(i, rb))
-                for tt in range(TOKEN_TILES):
-                    acc = accs[(n, tt)]
-                    if i == first_factor[rb]:
-                        res[(rb, tt)] = keep.tile([P, BLOCK], F32, name="res%d_%d" % (rb, tt))
+        def multiply(n, pending):
+            i, rb = GROUPS[n]
+            nr = P * len(rank_tiles(i, rb))
+            gs = passes(i, rb)
+            accs = []
+            for tt in range(TOKEN_TILES):
+                acc = psum_a.tile([P, BLOCK], F32, name="acc", tag="acc")
+                accs.append(acc)
+                for g in gs:
+                    nc.tensor.matmul_mx(
+                        out=acc[:, 0:nr],
+                        lhsT=zc[g][:, P * tt : P * tt + P].bitcast(FP8X4),
+                        lhsT_scale=zs[g][:, P * tt : P * tt + P],
+                        rhs=w_codes[(n, g)][:].bitcast(FP8X4),
+                        rhs_scale=w_scales[(n, g)][:],
+                        start=(g == gs[0]),
+                        stop=(g == gs[-1]),
+                    )
+            for tt in range(TOKEN_TILES):
+                acc = accs[tt]
+                if i == first_factor[rb]:
+                    rt = keep.tile([P, BLOCK], F32, name="res%d_%d" % (rb, tt))
+                    res[(rb, tt)] = rt
+                    nc.scalar.copy(out=rt[:], in_=acc[:])
+                else:
                     rt = res[(rb, tt)]
-                    for c0, width in cuts(n, tt):
-                        r0 = BLOCK - nr + c0
-                        if i != first_factor[rb]:
-                            nc.vector.scalar_tensor_tensor(
-                                out=rt[:, r0 : r0 + width],
-                                in0=acc[:, c0 : c0 + width],
-                                scalar=1.0,
-                                in1=rt[:, r0 : r0 + width],
-                                op0=ADD,
-                                op1=MULT,
-                            )
-                        elif rb == 0:
-                            nc.vector.tensor_copy(out=rt[:, r0 : r0 + width], in_=acc[:, c0 : c0 + width])
-                        else:
-                            nc.scalar.copy(out=rt[:, r0 : r0 + width], in_=acc[:, c0 : c0 + width])
-                        if i == last_factor[rb]:
-                            s0 = 0 if c0 == 0 else r0
-                            nc.sync.dma_start(
-                                out=out[P * tt : P * tt + P, BLOCK * rb + s0 : BLOCK * rb + r0 + width],
-                                in_=rt[:, s0 : r0 + width],
-                            )
-                    if served < len(pending):
-                        quantise(pending[served])
-                        served += 1
-            for bank in pending[served:]:
+                    nc.vector.scalar_tensor_tensor(
+                        out=rt[:, BLOCK - nr : BLOCK],
+                        in0=acc[:, 0:nr],
+                        scalar=1.0,
+                        in1=rt[:, BLOCK - nr : BLOCK],
+                        op0=ADD,
+                        op1=MULT,
+                    )
+                if i == last_factor[rb]:
+                    nc.sync.dma_start(out=out[P * tt : P * tt + P, BLOCK * rb : BLOCK * rb + BLOCK], in_=rt[:])
+                if tt < len(pending):
+                    quantise(pending[tt])
+            for bank in pending[TOKEN_TILES:]:
                 quantise(bank)
 
-        d_after = []
-        for n, (i, rb) in enumerate(GROUPS):
-            need = max([run_of_group[n]] + [run_of_z[g] for g in passes(i, rb)])
-            d_after.append(max(d_after[-1:] + [need + (1 if n == 0 else LAG)]))
-
         mask_run(0)
+        d_next = 0
         for k, bank_run in enumerate(runs):
             for bank in bank_run:
                 transpose_bank(bank)
-            if k > 0:
-                mask_run(k + 1)
+            mask_run(k + 1)
             for bank in bank_run:
                 copy_bank(bank)
             pending = [bank for bank in bank_run if bank[4]]
-            if k == 0:
+            ready = False
+            if d_next < len(GROUPS):
+                need = max([run_of_group[d_next]] + [run_of_z[g] for g in passes(*GROUPS[d_next])])
+                ready = need <= k - LAG
+            if ready:
+                multiply(d_next, pending)
+                d_next += 1
+            else:
                 for bank in pending:
                     quantise(bank)
-                pending = []
-                mask_run(1)
-            multiply([n for n in range(len(GROUPS)) if d_after[n] == k], pending)
-        multiply([n for n in range(len(GROUPS)) if d_after[n] >= len(runs)], [])
+        while d_next < len(GROUPS):
+            multiply(d_next, [])
+            d_next += 1

@@ -26,7 +26,7 @@ ALIVE = 4063232
 FLOPS = 2 * TOKENS * ALIVE
 BYTES = TOKENS * FEAT * 2 + TOKENS * RANKS * 4 + 2 * 3049344
 
-PINNED = True
+PINNED = False
 RUN = 4
 LAG = 2
 GROUPS = ((0, 0), (0, 1), (2, 1), (1, 1), (1, 0), (0, 2), (1, 2), (2, 2))
@@ -51,18 +51,6 @@ def alive_span(i, r):
     if LOWER[i]:
         return 0, P * (r + 1)
     return P * r, FEAT
-
-
-def group_window(i, rb):
-    if LOWER[i]:
-        return 0, BLOCK * (rb + 1)
-    lo = P * rank_tiles(i, rb)[0]
-    return lo, FEAT - lo
-
-
-def place(i, rb, j, c):
-    lo, width = group_window(i, rb)
-    return (BLOCK if LOWER[i] else 0) + j * width + c - lo
 
 
 def tile_cp_sparse_degree_lu_pa_kernel(tc, z, U_lo, masks_lo, out):
@@ -102,19 +90,16 @@ def tile_cp_sparse_degree_lu_pa_kernel(tc, z, U_lo, masks_lo, out):
                         in_=z[2 * h : 2 * h + 2, :, K_PASS * g : K_PASS * g + K_PASS].rearrange("t p c -> p t c"),
                     )
                     z_sb[(g, h)] = zt
-            rs = rank_tiles(i, rb)
-            ut = keep.tile([P, len(rs) * (group_window(i, rb)[1] + P)], BF16, name="u%d_%d" % (i, rb))
-            u_sb[(i, rb)] = ut
-            for j, r in enumerate(rs):
+            for r in rank_tiles(i, rb):
                 c0, c1 = tile_span(i, r)
                 a0, a1 = alive_span(i, r)
+                ut = keep.tile([P, c1 - c0], BF16, name="u%d_%d" % (i, r))
                 if a0 > c0:
-                    nc.vector.memset(ut[:, place(i, rb, j, c0) : place(i, rb, j, a0)].bitcast(I32), 0)
+                    nc.vector.memset(ut[:, 0 : a0 - c0].bitcast(I32), 0)
                 if a1 < c1:
-                    nc.vector.memset(ut[:, place(i, rb, j, a1) : place(i, rb, j, c1)].bitcast(I32), 0)
-                nc.sync.dma_start(
-                    out=ut[:, place(i, rb, j, a0) : place(i, rb, j, a1)], in_=U_lo[i, P * r : P * r + P, a0:a1]
-                )
+                    nc.vector.memset(ut[:, a1 - c0 : c1 - c0].bitcast(I32), 0)
+                nc.sync.dma_start(out=ut[:, a0 - c0 : a1 - c0], in_=U_lo[i, P * r : P * r + P, a0:a1])
+                u_sb[(i, r)] = ut
 
         banks = []
         for n, (i, rb) in enumerate(GROUPS):
@@ -171,13 +156,12 @@ def tile_cp_sparse_degree_lu_pa_kernel(tc, z, U_lo, masks_lo, out):
                 if kind == "w" and n not in masked:
                     masked.add(n)
                     i, rb = GROUPS[n]
-                    nj = len(rank_tiles(i, rb))
-                    width = group_window(i, rb)[1]
-                    d0 = width if LOWER[i] else 0
-                    diag = u_sb[(i, rb)][:].rearrange("p (j x) -> p j x", x=width + P)[:, :, d0 : d0 + P]
-                    nc.vector.tensor_tensor(
-                        out=diag, in0=diag, in1=tri[LOWER[i]][:].unsqueeze(1).to_broadcast([P, nj, P]), op=MULT
-                    )
+                    for r in rank_tiles(i, rb):
+                        d0 = P * r - tile_span(i, r)[0]
+                        ut = u_sb[(i, r)]
+                        nc.vector.tensor_tensor(
+                            out=ut[:, d0 : d0 + P], in0=ut[:, d0 : d0 + P], in1=tri[LOWER[i]][:], op=MULT
+                        )
 
         def transpose_bank(bank):
             kind, n, g, h, done = bank
@@ -193,9 +177,10 @@ def tile_cp_sparse_degree_lu_pa_kernel(tc, z, U_lo, masks_lo, out):
             rs = rank_tiles(i, rb)
             for plane, u in enumerate(alive_planes(i, rb, g, h)):
                 for a in range(2):
-                    w0 = place(i, rb, 2 * h + a, K_PASS * g + 256 * u) // 2
+                    r = rs[2 * h + a]
+                    w0 = (K_PASS * g + 256 * u - tile_span(i, r)[0]) // 2
                     nc.tensor.transpose(
-                        tp[:, plane, P * a : P * a + P], u_sb[(i, rb)][:].bitcast(F32)[:, w0 : w0 + P], ident[:]
+                        tp[:, plane, P * a : P * a + P], u_sb[(i, r)][:].bitcast(F32)[:, w0 : w0 + P], ident[:]
                     )
 
         def copy_bank(bank):

@@ -246,7 +246,10 @@ def tile_cp_sparse_degree_lu_pa_kernel(tc, z, U_lo, masks_lo, out):
                 if i == first_factor[rb]:
                     rt = keep.tile([P, BLOCK], F32, name="res%d_%d" % (rb, tt))
                     res[(rb, tt)] = rt
-                    nc.scalar.copy(out=rt[:], in_=acc[:])
+                    if tt % 2 == 0:
+                        nc.scalar.copy(out=rt[:], in_=acc[:])
+                    else:
+                        nc.vector.tensor_copy(out=rt[:], in_=acc[:])
                 else:
                     rt = res[(rb, tt)]
                     nc.vector.scalar_tensor_tensor(

from contextlib import ExitStack

import concourse.mybir as mybir
from concourse.masks import make_identity

F32 = mybir.dt.float32
BF16 = mybir.dt.bfloat16
U32 = mybir.dt.uint32
U8 = mybir.dt.uint8
I32 = mybir.dt.int32
FP8X4 = mybir.dt.float8_e4m3fn_x4
ADD = mybir.AluOpType.add
MULT = mybir.AluOpType.mult

P = 128
FEAT = 1536
RANKS = 1536
TOKENS = 512
K_PASS = 512
N_PASS = FEAT // K_PASS
BLOCK = 512
TOKEN_TILES = TOKENS // P
LOWER = (True, False, True)

ALIVE = 4063232
FLOPS = 2 * TOKENS * ALIVE
BYTES = TOKENS * FEAT * 2 + TOKENS * RANKS * 4 + 2 * 3049344

PINNED = False
RUN = 4
LAG = 2
GROUPS = ((0, 0), (0, 1), (2, 1), (1, 1), (1, 0), (0, 2), (1, 2), (2, 2))
Z_BEFORE = {0: 0, 1: 1, 3: 2}


def rank_tiles(i, rb):
    return [r for r in range(4 * rb, 4 * rb + 4) if r >= 2 * i]


def passes(i, rb):
    return list(range(0, rb + 1)) if LOWER[i] else list(range(rb, N_PASS))


def tile_span(i, r):
    if LOWER[i]:
        return 0, 256 * (r // 2 + 1)
    return 256 * (r // 2), FEAT


def alive_span(i, r):
    if LOWER[i]:
        return 0, P * (r + 1)
    return P * r, FEAT


def tile_cp_sparse_degree_lu_pa_kernel(tc, z, U_lo, masks_lo, out):
    nc = tc.nc
    first_factor = {}
    last_factor = {}
    for i, rb in GROUPS:
        if rb not in first_factor:
            first_factor[rb] = i
        last_factor[rb] = i

    with ExitStack() as ctx:
        keep = ctx.enter_context(tc.tile_pool(name="keep", bufs=1))
        stage = ctx.enter_context(tc.tile_pool(name="stage", bufs=4))
        psum_t = ctx.enter_context(tc.psum_pool(name="psum_t", bufs=4))
        psum_a = ctx.enter_context(tc.psum_pool(name="psum_a", bufs=4))
        if PINNED:
            ctx.enter_context(tc.manual_schedule())

        ident = keep.tile([P, P], F32, name="ident")
        make_identity(nc, ident[:])

        tri = {}
        for lower, i, r in ((True, 0, 0), (False, 1, 2)):
            mt = keep.tile([P, P], BF16, name="tri%d" % i)
            nc.sync.dma_start(out=mt[:], in_=masks_lo[i, P * r : P * r + P, P * r : P * r + P])
            tri[lower] = mt
        z_sb = {}
        u_sb = {}
        for n, (i, rb) in enumerate(GROUPS):
            if n in Z_BEFORE:
                g = Z_BEFORE[n]
                for h in range(2):
                    zt = keep.tile([P, 2, K_PASS], BF16, name="z%d_%d" % (g, h))
                    nc.sync.dma_start(
                        out=zt[:],
                        in_=z[2 * h : 2 * h + 2, :, K_PASS * g : K_PASS * g + K_PASS].rearrange("t p c -> p t c"),
                    )
                    z_sb[(g, h)] = zt
            for r in rank_tiles(i, rb):
                c0, c1 = tile_span(i, r)
                a0, a1 = alive_span(i, r)
                ut = keep.tile([P, c1 - c0], BF16, name="u%d_%d" % (i, r))
                if a0 > c0:
                    nc.vector.memset(ut[:, 0 : a0 - c0].bitcast(I32), 0)
                if a1 < c1:
                    nc.vector.memset(ut[:, a1 - c0 : c1 - c0].bitcast(I32), 0)
                nc.sync.dma_start(out=ut[:, a0 - c0 : a1 - c0], in_=U_lo[i, P * r : P * r + P, a0:a1])
                u_sb[(i, r)] = ut

        banks = []
        for n, (i, rb) in enumerate(GROUPS):
            if n in Z_BEFORE:
                banks.append(("z", n, Z_BEFORE[n], 0, False))
                banks.append(("z", n, Z_BEFORE[n], 1, True))
            gs = passes(i, rb)
            if not LOWER[i]:
                gs = list(reversed(gs))
            nb = len(rank_tiles(i, rb)) // 2
            for g in gs:
                for h in range(nb):
                    banks.append(("w", n, g, h, h == nb - 1))
        runs = [banks[k : k + RUN] for k in range(0, len(banks), RUN)]
        run_of_group = {}
        run_of_z = {}
        for k, bank_run in enumerate(runs):
            for kind, n, g, h, done in bank_run:
                if kind == "z":
                    run_of_z[g] = k
                else:
                    run_of_group[n] = k

        def alive_planes(i, rb, g, h):
            rs = rank_tiles(i, rb)
            c0, c1 = tile_span(i, rs[2 * h])
            d0, d1 = tile_span(i, rs[2 * h + 1])
            return [u for u in range(2) if min(c0, d0) <= K_PASS * g + 256 * u < max(c1, d1)]

        fixed_gr = {}
        for n, (i, rb) in enumerate(GROUPS):
            nb = len(rank_tiles(i, rb)) // 2
            for g in passes(i, rb):
                for h in range(nb):
                    if len(alive_planes(i, rb, g, h)) == 1:
                        gt = keep.tile([P, 1024 * nb], BF16, name="gf%d_%d" % (n, g), align_bytes=64)
                        nc.vector.memset(gt[:, 1024 * h : 1024 * h + 1024].bitcast(I32), 0)
                        fixed_gr[(n, g)] = gt

        zg = {}
        zc = {}
        zs = {}
        gr_of = {}
        w_codes = {}
        w_scales = {}
        res = {}
        tp_of = {}
        masked = set()

        def mask_run(k):
            if k >= len(runs):
                return
            for kind, n, g, h, done in runs[k]:
                if kind == "w" and n not in masked:
                    masked.add(n)
                    i, rb = GROUPS[n]
                    for r in rank_tiles(i, rb):
                        d0 = P * r - tile_span(i, r)[0]
                        ut = u_sb[(i, r)]
                        nc.vector.tensor_tensor(
                            out=ut[:, d0 : d0 + P], in0=ut[:, d0 : d0 + P], in1=tri[LOWER[i]][:], op=MULT
                        )

        def transpose_bank(bank):
            kind, n, g, h, done = bank
            tp = psum_t.tile([P, 2, 256], F32, name="tp", tag="tp")
            tp_of[bank] = tp
            if kind == "z":
                for a in range(2):
                    words = z_sb[(g, h)][:, a, :].bitcast(F32)
                    for u in range(2):
                        nc.tensor.transpose(tp[:, u, P * a : P * a + P], words[:, P * u : P * u + P], ident[:])
                return
            i, rb = GROUPS[n]
            rs = rank_tiles(i, rb)
            for plane, u in enumerate(alive_planes(i, rb, g, h)):
                for a in range(2):
                    r = rs[2 * h + a]
                    w0 = (K_PASS * g + 256 * u - tile_span(i, r)[0]) // 2
                    nc.tensor.transpose(
                        tp[:, plane, P * a : P * a + P], u_sb[(i, r)][:].bitcast(F32)[:, w0 : w0 + P], ident[:]
                    )

        def copy_bank(bank):
            kind, n, g, h, done = bank
            tp = tp_of[bank]
            if kind == "z":
                if h == 0:
                    zg[g] = keep.tile([P, 4 * TOKENS], BF16, name="zg%d" % g, align_bytes=64)
                dst = zg[g][:].bitcast(F32).rearrange("p (r u) -> p r u", u=2)
                nc.scalar.copy(out=dst[:, 256 * h : 256 * h + 256, :], in_=tp[:].rearrange("p u r -> p r u"))
                return
            i, rb = GROUPS[n]
            nb = len(rank_tiles(i, rb)) // 2
            if h == 0:
                if (n, g) in fixed_gr:
                    gr_of[(n, g)] = fixed_gr[(n, g)]
                else:
                    gr_of[(n, g)] = stage.tile([P, 1024 * nb], BF16, name="gr", tag="gr", align_bytes=64)
            dst = gr_of[(n, g)][:].bitcast(F32).rearrange("p (r u) -> p r u", u=2)
            planes = alive_planes(i, rb, g, h)
            if len(planes) == 2:
                nc.scalar.copy(out=dst[:, 256 * h : 256 * h + 256, :], in_=tp[:].rearrange("p u r -> p r u"))
            else:
                u = planes[0]
                nc.scalar.copy(
                    out=dst[:, 256 * h : 256 * h + 256, u : u + 1], in_=tp[:, 0:1, :].rearrange("p u r -> p r u")
                )

        def quantise(bank):
            kind, n, g, h, done = bank
            if kind == "z":
                zc[g] = keep.tile([P, TOKENS], U32, name="zc%d" % g, align_bytes=64)
                zs[g] = keep.tile([P, TOKENS], U8, name="zs%d" % g, align_bytes=64)
                nc.vector.quantize_mx(out=zc[g][:].bitcast(FP8X4), scales=zs[g][:], in_=zg[g][:])
                return
            nr = P * len(rank_tiles(*GROUPS[n]))
            wc = keep.tile([P, nr], U32, name="wc%d_%d" % (n, g), align_bytes=64)
            ws = keep.tile([P, nr], U8, name="ws%d_%d" % (n, g), align_bytes=64)
            nc.vector.quantize_mx(out=wc[:].bitcast(FP8X4), scales=ws[:], in_=gr_of[(n, g)][:])
            w_codes[(n, g)] = wc
            w_scales[(n, g)] = ws

        def multiply(n, pending):
            i, rb = GROUPS[n]
            nr = P * len(rank_tiles(i, rb))
            gs = passes(i, rb)
            accs = []
            for tt in range(TOKEN_TILES):
                acc = psum_a.tile([P, BLOCK], F32, name="acc", tag="acc")
                accs.append(acc)
                for g in gs:
                    nc.tensor.matmul_mx(
                        out=acc[:, 0:nr],
                        lhsT=zc[g][:, P * tt : P * tt + P].bitcast(FP8X4),
                        lhsT_scale=zs[g][:, P * tt : P * tt + P],
                        rhs=w_codes[(n, g)][:].bitcast(FP8X4),
                        rhs_scale=w_scales[(n, g)][:],
                        start=(g == gs[0]),
                        stop=(g == gs[-1]),
                    )
            for tt in range(TOKEN_TILES):
                acc = accs[tt]
                if i == first_factor[rb]:
                    rt = keep.tile([P, BLOCK], F32, name="res%d_%d" % (rb, tt))
                    res[(rb, tt)] = rt
                    if tt % 2 == 0:
                        nc.scalar.copy(out=rt[:], in_=acc[:])
                    else:
                        nc.vector.tensor_copy(out=rt[:], in_=acc[:])
                else:
                    rt = res[(rb, tt)]
                    nc.vector.scalar_tensor_tensor(
                        out=rt[:, BLOCK - nr : BLOCK],
                        in0=acc[:, 0:nr],
                        scalar=1.0,
                        in1=rt[:, BLOCK - nr : BLOCK],
                        op0=ADD,
                        op1=MULT,
                    )
                if i == last_factor[rb]:
                    nc.sync.dma_start(out=out[P * tt : P * tt + P, BLOCK * rb : BLOCK * rb + BLOCK], in_=rt[:])
                if tt < len(pending):
                    quantise(pending[tt])
            for bank in pending[TOKEN_TILES:]:
                quantise(bank)

        mask_run(0)
        d_next = 0
        for k, bank_run in enumerate(runs):
            for bank in bank_run:
                transpose_bank(bank)
            mask_run(k + 1)
            for bank in bank_run:
                copy_bank(bank)
            pending = [bank for bank in bank_run if bank[4]]
            ready = False
            if d_next < len(GROUPS):
                need = max([run_of_group[d_next]] + [run_of_z[g] for g in passes(*GROUPS[d_next])])
                ready = need <= k - LAG
            if ready:
                multiply(d_next, pending)
                d_next += 1
            else:
                for bank in pending:
                    quantise(bank)
        while d_next < len(GROUPS):
            multiply(d_next, [])
            d_next += 1
